import numpy as np
import ml_dtypes


def mxq(x, axis, fmt="e4m3"):
    dtype, down = {"e4m3": (ml_dtypes.float8_e4m3fn, 7), "e5m2": (ml_dtypes.float8_e5m2, 14)}[fmt]
    v = np.moveaxis(np.asarray(x, np.float32).astype(ml_dtypes.bfloat16).astype(np.float64), axis, -1)
    blocks = v.reshape(v.shape[:-1] + (-1, 32))
    amax = np.abs(blocks).max(-1, keepdims=True)
    byte = np.maximum(np.where(amax > 0, np.frexp(amax)[1] - 1 + 127, 0) - down, 1)
    scale = np.exp2(byte - 127.0)
    codes = (blocks / scale).astype(np.float32).astype(dtype).astype(np.float64)
    return np.moveaxis((codes * scale).reshape(v.shape), -1, axis)


WIDE = False


def mx_kscale(k):
    if not WIDE:
        return np.ones(k)
    levels = np.array([10, -10, 5, -5, 0])
    a = np.random.permutation(np.resize(levels, k // 512 * 4)).reshape(k // 512, 4)
    idx = np.arange(k)
    return np.exp2(a[idx // 512, idx % 128 // 32])


BF16 = ml_dtypes.bfloat16


def bf(x):
    return np.asarray(x, np.float32).astype(BF16)


def f64(x):
    return np.asarray(x).astype(np.float64)


B, H, L, E, QD = 16, 1, 128, 2048, 128


def setup_inputs():
    s = mx_kscale(E)
    return {"x": bf(np.random.standard_normal((B, H, L, E)) * s),
            "Wk": bf(np.random.standard_normal((QD, E)) * 0.3 / np.sqrt(E) / s),
            "bk": bf(0.1 + 0.1 * np.random.standard_normal(QD)),
            "Wv": bf(np.random.standard_normal((QD, E)) * 0.3 / np.sqrt(E) / s),
            "bv": bf(0.1 + 0.1 * np.random.standard_normal(QD))}


def reference(x, Wk, bk, Wv, bv):
    xq = mxq(f64(x), 3, "e4m3")
    K = (xq @ mxq(f64(Wk), 1, "e4m3").T) + f64(bk)
    V = (xq @ mxq(f64(Wv), 1, "e4m3").T) + f64(bv)
    return K * V

@@ -1,0 +1,149 @@
+from contextlib import ExitStack
+
+import concourse.mybir as mybir
+from concourse.masks import make_identity
+
+F32 = mybir.dt.float32
+BF16 = mybir.dt.bfloat16
+U32 = mybir.dt.uint32
+U8 = mybir.dt.uint8
+FP8X4 = mybir.dt.float8_e4m3fn_x4
+ADD = mybir.AluOpType.add
+MULT = mybir.AluOpType.mult
+
+P = 128
+ROWS = 16 * 1 * 128
+E = 2048
+QD = 128
+K_PASS = 4 * P
+PASSES = E // K_PASS
+WORDS = E // 2
+BANK = 512
+TRANSPOSES_PER_BANK = BANK // P
+BANKS_PER_TILE = WORDS // BANK
+PASSES_PER_BANK = PASSES // BANKS_PER_TILE
+ROW_TILES = ROWS // P
+TILES_PER_ROUND = BANK // (2 * QD)
+ROUNDS = ROW_TILES // TILES_PER_ROUND
+
+FLOPS = 2 * ROWS * E * 2 * QD
+
+
+def transpose_rows(nc, banks, identity, words, copy, grouped_words):
+    for h in range(BANKS_PER_TILE):
+        bank = banks.tile([P, BANK], F32)
+        for j in range(TRANSPOSES_PER_BANK):
+            first = (h * TRANSPOSES_PER_BANK + j) * P
+            nc.tensor.transpose(bank[:, j * P : (j + 1) * P], words[:, first : first + P], identity[:])
+        copy(
+            out=grouped_words[:, h * PASSES_PER_BANK : (h + 1) * PASSES_PER_BANK, :, :],
+            in_=bank[:].rearrange("p (g u r) -> p g r u", g=PASSES_PER_BANK, u=2),
+        )
+
+
+def tile_parallelretention_pa_kernel(tc, x, Wk, bk, Wv, bv, out):
+    nc = tc.nc
+    x_rows = x.flatten_outer_dims().rearrange("(p t) e -> p (t e)", t=ROW_TILES)
+    out_rows = out.flatten_outer_dims().rearrange("(p t) q -> p (t q)", t=ROW_TILES)
+
+    with ExitStack() as ctx:
+        const = ctx.enter_context(tc.tile_pool(name="const", bufs=1))
+        x_pool = ctx.enter_context(tc.tile_pool(name="x_pool", bufs=ROUNDS))
+        stage = ctx.enter_context(tc.tile_pool(name="stage", bufs=2 * TILES_PER_ROUND))
+        operands = ctx.enter_context(tc.tile_pool(name="operands", bufs=3 * TILES_PER_ROUND))
+        results = ctx.enter_context(tc.tile_pool(name="results", bufs=3))
+        banks = ctx.enter_context(tc.psum_pool(name="banks", bufs=6))
+        sums = ctx.enter_context(tc.psum_pool(name="sums", bufs=2))
+        ctx.enter_context(tc.manual_schedule())
+
+        wk_sb = const.tile([P, E], BF16)
+        nc.sync.dma_start(out=wk_sb[:], in_=Wk)
+        wv_sb = const.tile([P, E], BF16)
+        nc.sync.dma_start(out=wv_sb[:], in_=Wv)
+        x_tiles = []
+        for i in range(ROUNDS):
+            x_sb = x_pool.tile([P, TILES_PER_ROUND * E], BF16)
+            nc.sync.dma_start(
+                out=x_sb[:], in_=x_rows[:, i * TILES_PER_ROUND * E : (i + 1) * TILES_PER_ROUND * E]
+            )
+            x_tiles.append(x_sb)
+
+        identity = const.tile([P, P], F32)
+        make_identity(nc, identity[:])
+
+        bias_rows = const.tile([P, 2 * QD], BF16)
+        nc.vector.memset(bias_rows[:], 0.0)
+        nc.scalar.dma_start(out=bias_rows[0:1, 0:QD], in_=bk.rearrange("(o q) -> o q", o=1))
+        nc.scalar.dma_start(out=bias_rows[0:1, QD : 2 * QD], in_=bv.rearrange("(o q) -> o q", o=1))
+        ones = const.tile([P, P], BF16)
+        nc.vector.memset(ones[:], 1.0)
+        bias_sum = sums.tile([P, BANK], F32, tag="acc")
+        nc.tensor.matmul(out=bias_sum[:, 0 : 2 * QD], lhsT=ones[:], rhs=bias_rows[:], start=True, stop=True)
+        bias = const.tile([P, BANK], F32)
+        for t in range(TILES_PER_ROUND):
+            nc.vector.tensor_copy(out=bias[:, t * 2 * QD : (t + 1) * 2 * QD], in_=bias_sum[:, 0 : 2 * QD])
+
+        w_grouped = const.tile([P, PASSES * 2 * QD * 4], BF16, align_bytes=64)
+        w_words = w_grouped[:].bitcast(F32).rearrange("p (g n u) -> p g n u", g=PASSES, u=2)
+        transpose_rows(nc, banks, identity, wk_sb[:].bitcast(F32), nc.scalar.copy, w_words[:, :, 0:QD, :])
+        transpose_rows(
+            nc, banks, identity, wv_sb[:].bitcast(F32), nc.vector.tensor_copy, w_words[:, :, QD : 2 * QD, :]
+        )
+        w_codes = const.tile([P, PASSES * 2 * QD], U32, align_bytes=64)
+        w_scales = const.tile([P, PASSES * 2 * QD], U8, align_bytes=64)
+        nc.vector.quantize_mx(out=w_codes[:].bitcast(FP8X4), scales=w_scales[:], in_=w_grouped[:])
+
+        def transpose_and_quantise(i):
+            pairs = []
+            for t in range(TILES_PER_ROUND):
+                grouped = stage.tile([P, PASSES * P * 4], BF16, align_bytes=64)
+                transpose_rows(
+                    nc,
+                    banks,
+                    identity,
+                    x_tiles[i][:].bitcast(F32)[:, t * WORDS : (t + 1) * WORDS],
+                    nc.scalar.copy,
+                    grouped[:].bitcast(F32).rearrange("p (g r u) -> p g r u", g=PASSES, u=2),
+                )
+                codes = operands.tile([P, PASSES * P], U32, align_bytes=64)
+                scales = operands.tile([P, PASSES * P], U8, align_bytes=64)
+                nc.vector.quantize_mx(out=codes[:].bitcast(FP8X4), scales=scales[:], in_=grouped[:])
+                pairs.append((codes, scales))
+            return pairs
+
+        def multiply_and_store(i, pairs):
+            acc = sums.tile([P, BANK], F32, tag="acc")
+            for t in range(TILES_PER_ROUND):
+                codes, scales = pairs[t]
+                for g in range(PASSES):
+                    rows = slice(g * P, (g + 1) * P)
+                    cols = slice(g * 2 * QD, (g + 1) * 2 * QD)
+                    nc.tensor.matmul_mx(
+                        out=acc[:, t * 2 * QD : (t + 1) * 2 * QD],
+                        lhsT=codes[:, rows].bitcast(FP8X4),
+                        lhsT_scale=scales[:, rows],
+                        rhs=w_codes[:, cols].bitcast(FP8X4),
+                        rhs_scale=w_scales[:, cols],
+                        start=(g == 0),
+                        stop=(g == PASSES - 1),
+                    )
+            k_and_v = results.tile([P, BANK], F32)
+            nc.vector.tensor_tensor(out=k_and_v[:], in0=acc[:], in1=bias[:], op=ADD)
+            halves = k_and_v[:].rearrange("p (t c q) -> p t c q", t=TILES_PER_ROUND, c=2)
+            kv = results.tile([P, TILES_PER_ROUND * QD], F32)
+            nc.vector.tensor_tensor(
+                out=kv[:].rearrange("p (t q) -> p t q", t=TILES_PER_ROUND),
+                in0=halves[:, :, 0, :],
+                in1=halves[:, :, 1, :],
+                op=MULT,
+            )
+            nc.sync.dma_start(
+                out=out_rows[:, i * TILES_PER_ROUND * QD : (i + 1) * TILES_PER_ROUND * QD], in_=kv[:]
+            )
+
+        waiting = transpose_and_quantise(0)
+        for i in range(1, ROUNDS):
+            following = transpose_and_quantise(i)
+            multiply_and_store(i - 1, waiting)
+            waiting = following
+        multiply_and_store(ROUNDS - 1, waiting)

@@ -48,7 +48,7 @@ def tile_parallelretention_pa_kernel(tc, x, Wk, bk, Wv, bv, out):
 
     with ExitStack() as ctx:
         const = ctx.enter_context(tc.tile_pool(name="const", bufs=1))
-        x_pool = ctx.enter_context(tc.tile_pool(name="x_pool", bufs=ROUNDS))
+        x_pool = ctx.enter_context(tc.tile_pool(name="x_pool", bufs=ROW_TILES))
         stage = ctx.enter_context(tc.tile_pool(name="stage", bufs=2 * TILES_PER_ROUND))
         operands = ctx.enter_context(tc.tile_pool(name="operands", bufs=3 * TILES_PER_ROUND))
         results = ctx.enter_context(tc.tile_pool(name="results", bufs=3))
@@ -56,32 +56,24 @@ def tile_parallelretention_pa_kernel(tc, x, Wk, bk, Wv, bv, out):
         sums = ctx.enter_context(tc.psum_pool(name="sums", bufs=2))
         ctx.enter_context(tc.manual_schedule())
 
+        bias_rows = const.tile([P, 2 * QD], BF16)
+        nc.vector.memset(bias_rows[:], 0.0)
+        nc.scalar.dma_start(out=bias_rows[0:1, 0:QD], in_=bk.rearrange("(o q) -> o q", o=1))
+        nc.scalar.dma_start(out=bias_rows[0:1, QD : 2 * QD], in_=bv.rearrange("(o q) -> o q", o=1))
         wk_sb = const.tile([P, E], BF16)
         nc.sync.dma_start(out=wk_sb[:], in_=Wk)
         wv_sb = const.tile([P, E], BF16)
         nc.sync.dma_start(out=wv_sb[:], in_=Wv)
         x_tiles = []
-        for i in range(ROUNDS):
-            x_sb = x_pool.tile([P, TILES_PER_ROUND * E], BF16)
-            nc.sync.dma_start(
-                out=x_sb[:], in_=x_rows[:, i * TILES_PER_ROUND * E : (i + 1) * TILES_PER_ROUND * E]
-            )
+        for t in range(ROW_TILES):
+            x_sb = x_pool.tile([P, E], BF16)
+            nc.sync.dma_start(out=x_sb[:], in_=x_rows[:, t * E : (t + 1) * E])
             x_tiles.append(x_sb)
 
         identity = const.tile([P, P], F32)
         make_identity(nc, identity[:])
-
-        bias_rows = const.tile([P, 2 * QD], BF16)
-        nc.vector.memset(bias_rows[:], 0.0)
-        nc.scalar.dma_start(out=bias_rows[0:1, 0:QD], in_=bk.rearrange("(o q) -> o q", o=1))
-        nc.scalar.dma_start(out=bias_rows[0:1, QD : 2 * QD], in_=bv.rearrange("(o q) -> o q", o=1))
         ones = const.tile([P, P], BF16)
         nc.vector.memset(ones[:], 1.0)
-        bias_sum = sums.tile([P, BANK], F32, tag="acc")
-        nc.tensor.matmul(out=bias_sum[:, 0 : 2 * QD], lhsT=ones[:], rhs=bias_rows[:], start=True, stop=True)
-        bias = const.tile([P, BANK], F32)
-        for t in range(TILES_PER_ROUND):
-            nc.vector.tensor_copy(out=bias[:, t * 2 * QD : (t + 1) * 2 * QD], in_=bias_sum[:, 0 : 2 * QD])
 
         w_grouped = const.tile([P, PASSES * 2 * QD * 4], BF16, align_bytes=64)
         w_words = w_grouped[:].bitcast(F32).rearrange("p (g n u) -> p g n u", g=PASSES, u=2)
@@ -93,6 +85,12 @@ def tile_parallelretention_pa_kernel(tc, x, Wk, bk, Wv, bv, out):
         w_scales = const.tile([P, PASSES * 2 * QD], U8, align_bytes=64)
         nc.vector.quantize_mx(out=w_codes[:].bitcast(FP8X4), scales=w_scales[:], in_=w_grouped[:])
 
+        bias_sum = sums.tile([P, BANK], F32, tag="acc")
+        nc.tensor.matmul(out=bias_sum[:, 0 : 2 * QD], lhsT=ones[:], rhs=bias_rows[:], start=True, stop=True)
+        bias = const.tile([P, BANK], F32)
+        for t in range(TILES_PER_ROUND):
+            nc.vector.tensor_copy(out=bias[:, t * 2 * QD : (t + 1) * 2 * QD], in_=bias_sum[:, 0 : 2 * QD])
+
         def transpose_and_quantise(i):
             pairs = []
             for t in range(TILES_PER_ROUND):
@@ -101,7 +99,7 @@ def tile_parallelretention_pa_kernel(tc, x, Wk, bk, Wv, bv, out):
                     nc,
                     banks,
                     identity,
-                    x_tiles[i][:].bitcast(F32)[:, t * WORDS : (t + 1) * WORDS],
+                    x_tiles[i * TILES_PER_ROUND + t][:].bitcast(F32),
                     nc.scalar.copy,
                     grouped[:].bitcast(F32).rearrange("p (g r u) -> p g r u", g=PASSES, u=2),
                 )

@@ -48,10 +48,11 @@ def tile_parallelretention_pa_kernel(tc, x, Wk, bk, Wv, bv, out):
 
     with ExitStack() as ctx:
         const = ctx.enter_context(tc.tile_pool(name="const", bufs=1))
-        x_pool = ctx.enter_context(tc.tile_pool(name="x_pool", bufs=ROW_TILES))
+        x_pool = ctx.enter_context(tc.tile_pool(name="x_pool", bufs=ROUNDS))
         stage = ctx.enter_context(tc.tile_pool(name="stage", bufs=2 * TILES_PER_ROUND))
         operands = ctx.enter_context(tc.tile_pool(name="operands", bufs=3 * TILES_PER_ROUND))
         results = ctx.enter_context(tc.tile_pool(name="results", bufs=3))
+        products = ctx.enter_context(tc.tile_pool(name="products", bufs=ROUNDS))
         banks = ctx.enter_context(tc.psum_pool(name="banks", bufs=6))
         sums = ctx.enter_context(tc.psum_pool(name="sums", bufs=2))
         ctx.enter_context(tc.manual_schedule())
@@ -65,9 +66,11 @@ def tile_parallelretention_pa_kernel(tc, x, Wk, bk, Wv, bv, out):
         wv_sb = const.tile([P, E], BF16)
         nc.sync.dma_start(out=wv_sb[:], in_=Wv)
         x_tiles = []
-        for t in range(ROW_TILES):
-            x_sb = x_pool.tile([P, E], BF16)
-            nc.sync.dma_start(out=x_sb[:], in_=x_rows[:, t * E : (t + 1) * E])
+        for i in range(ROUNDS):
+            x_sb = x_pool.tile([P, TILES_PER_ROUND * E], BF16)
+            nc.sync.dma_start(
+                out=x_sb[:], in_=x_rows[:, i * TILES_PER_ROUND * E : (i + 1) * TILES_PER_ROUND * E]
+            )
             x_tiles.append(x_sb)
 
         identity = const.tile([P, P], F32)
@@ -99,7 +102,7 @@ def tile_parallelretention_pa_kernel(tc, x, Wk, bk, Wv, bv, out):
                     nc,
                     banks,
                     identity,
-                    x_tiles[i * TILES_PER_ROUND + t][:].bitcast(F32),
+                    x_tiles[i][:].bitcast(F32)[:, t * WORDS : (t + 1) * WORDS],
                     nc.scalar.copy,
                     grouped[:].bitcast(F32).rearrange("p (g r u) -> p g r u", g=PASSES, u=2),
                 )
@@ -128,7 +131,7 @@ def tile_parallelretention_pa_kernel(tc, x, Wk, bk, Wv, bv, out):
             k_and_v = results.tile([P, BANK], F32)
             nc.vector.tensor_tensor(out=k_and_v[:], in0=acc[:], in1=bias[:], op=ADD)
             halves = k_and_v[:].rearrange("p (t c q) -> p t c q", t=TILES_PER_ROUND, c=2)
-            kv = results.tile([P, TILES_PER_ROUND * QD], F32)
+            kv = products.tile([P, TILES_PER_ROUND * QD], F32)
             nc.vector.tensor_tensor(
                 out=kv[:].rearrange("p (t q) -> p t q", t=TILES_PER_ROUND),
                 in0=halves[:, :, 0, :],

@@ -25,6 +25,7 @@ PASSES_PER_BANK = PASSES // BANKS_PER_TILE
 ROW_TILES = ROWS // P
 TILES_PER_ROUND = BANK // (2 * QD)
 ROUNDS = ROW_TILES // TILES_PER_ROUND
+LAG = 2
 
 FLOPS = 2 * ROWS * E * 2 * QD
 
@@ -46,9 +47,11 @@ def tile_parallelretention_pa_kernel(tc, x, Wk, bk, Wv, bv, out):
     x_rows = x.flatten_outer_dims().rearrange("(p t) e -> p (t e)", t=ROW_TILES)
     out_rows = out.flatten_outer_dims().rearrange("(p t) q -> p (t q)", t=ROW_TILES)
 
+    tile_groups = [[0], [1], [2], [3]] + [[t, t + 1] for t in range(4, ROW_TILES, 2)]
+
     with ExitStack() as ctx:
         const = ctx.enter_context(tc.tile_pool(name="const", bufs=1))
-        x_pool = ctx.enter_context(tc.tile_pool(name="x_pool", bufs=ROUNDS))
+        x_pool = ctx.enter_context(tc.tile_pool(name="x_pool", bufs=1))
         stage = ctx.enter_context(tc.tile_pool(name="stage", bufs=2 * TILES_PER_ROUND))
         operands = ctx.enter_context(tc.tile_pool(name="operands", bufs=3 * TILES_PER_ROUND))
         results = ctx.enter_context(tc.tile_pool(name="results", bufs=3))
@@ -61,17 +64,20 @@ def tile_parallelretention_pa_kernel(tc, x, Wk, bk, Wv, bv, out):
         nc.vector.memset(bias_rows[:], 0.0)
         nc.scalar.dma_start(out=bias_rows[0:1, 0:QD], in_=bk.rearrange("(o q) -> o q", o=1))
         nc.scalar.dma_start(out=bias_rows[0:1, QD : 2 * QD], in_=bv.rearrange("(o q) -> o q", o=1))
+        warm_in = const.tile([P, 1], F32)
+        nc.vector.memset(warm_in[:], 0.0)
+        warm_out = const.tile([P, 1], F32)
+        nc.scalar.copy(out=warm_out[:], in_=warm_in[:])
         wk_sb = const.tile([P, E], BF16)
         nc.sync.dma_start(out=wk_sb[:], in_=Wk)
         wv_sb = const.tile([P, E], BF16)
         nc.sync.dma_start(out=wv_sb[:], in_=Wv)
-        x_tiles = []
-        for i in range(ROUNDS):
-            x_sb = x_pool.tile([P, TILES_PER_ROUND * E], BF16)
-            nc.sync.dma_start(
-                out=x_sb[:], in_=x_rows[:, i * TILES_PER_ROUND * E : (i + 1) * TILES_PER_ROUND * E]
-            )
-            x_tiles.append(x_sb)
+        x_words = {}
+        for group in tile_groups:
+            x_sb = x_pool.tile([P, len(group) * E], BF16, tag="x%d" % group[0])
+            nc.sync.dma_start(out=x_sb[:], in_=x_rows[:, group[0] * E : (group[-1] + 1) * E])
+            for j, t in enumerate(group):
+                x_words[t] = x_sb[:].bitcast(F32)[:, j * WORDS : (j + 1) * WORDS]
 
         identity = const.tile([P, P], F32)
         make_identity(nc, identity[:])
@@ -94,40 +100,37 @@ def tile_parallelretention_pa_kernel(tc, x, Wk, bk, Wv, bv, out):
         for t in range(TILES_PER_ROUND):
             nc.vector.tensor_copy(out=bias[:, t * 2 * QD : (t + 1) * 2 * QD], in_=bias_sum[:, 0 : 2 * QD])
 
-        def transpose_and_quantise(i):
-            pairs = []
-            for t in range(TILES_PER_ROUND):
-                grouped = stage.tile([P, PASSES * P * 4], BF16, align_bytes=64)
-                transpose_rows(
-                    nc,
-                    banks,
-                    identity,
-                    x_tiles[i][:].bitcast(F32)[:, t * WORDS : (t + 1) * WORDS],
-                    nc.scalar.copy,
-                    grouped[:].bitcast(F32).rearrange("p (g r u) -> p g r u", g=PASSES, u=2),
-                )
-                codes = operands.tile([P, PASSES * P], U32, align_bytes=64)
-                scales = operands.tile([P, PASSES * P], U8, align_bytes=64)
-                nc.vector.quantize_mx(out=codes[:].bitcast(FP8X4), scales=scales[:], in_=grouped[:])
-                pairs.append((codes, scales))
-            return pairs
+        def transpose_and_quantise(t):
+            grouped = stage.tile([P, PASSES * P * 4], BF16, align_bytes=64)
+            transpose_rows(
+                nc,
+                banks,
+                identity,
+                x_words[t],
+                nc.scalar.copy,
+                grouped[:].bitcast(F32).rearrange("p (g r u) -> p g r u", g=PASSES, u=2),
+            )
+            codes = operands.tile([P, PASSES * P], U32, align_bytes=64)
+            scales = operands.tile([P, PASSES * P], U8, align_bytes=64)
+            nc.vector.quantize_mx(out=codes[:].bitcast(FP8X4), scales=scales[:], in_=grouped[:])
+            return codes, scales
 
-        def multiply_and_store(i, pairs):
-            acc = sums.tile([P, BANK], F32, tag="acc")
-            for t in range(TILES_PER_ROUND):
-                codes, scales = pairs[t]
-                for g in range(PASSES):
-                    rows = slice(g * P, (g + 1) * P)
-                    cols = slice(g * 2 * QD, (g + 1) * 2 * QD)
-                    nc.tensor.matmul_mx(
-                        out=acc[:, t * 2 * QD : (t + 1) * 2 * QD],
-                        lhsT=codes[:, rows].bitcast(FP8X4),
-                        lhsT_scale=scales[:, rows],
-                        rhs=w_codes[:, cols].bitcast(FP8X4),
-                        rhs_scale=w_scales[:, cols],
-                        start=(g == 0),
-                        stop=(g == PASSES - 1),
-                    )
+        def multiply(acc, t, codes, scales):
+            half = t % TILES_PER_ROUND
+            for g in range(PASSES):
+                rows = slice(g * P, (g + 1) * P)
+                cols = slice(g * 2 * QD, (g + 1) * 2 * QD)
+                nc.tensor.matmul_mx(
+                    out=acc[:, half * 2 * QD : (half + 1) * 2 * QD],
+                    lhsT=codes[:, rows].bitcast(FP8X4),
+                    lhsT_scale=scales[:, rows],
+                    rhs=w_codes[:, cols].bitcast(FP8X4),
+                    rhs_scale=w_scales[:, cols],
+                    start=(g == 0),
+                    stop=(g == PASSES - 1),
+                )
+
+        def finish(i, acc):
             k_and_v = results.tile([P, BANK], F32)
             nc.vector.tensor_tensor(out=k_and_v[:], in0=acc[:], in1=bias[:], op=ADD)
             halves = k_and_v[:].rearrange("p (t c q) -> p t c q", t=TILES_PER_ROUND, c=2)
@@ -142,9 +145,19 @@ def tile_parallelretention_pa_kernel(tc, x, Wk, bk, Wv, bv, out):
                 out=out_rows[:, i * TILES_PER_ROUND * QD : (i + 1) * TILES_PER_ROUND * QD], in_=kv[:]
             )
 
-        waiting = transpose_and_quantise(0)
-        for i in range(1, ROUNDS):
-            following = transpose_and_quantise(i)
-            multiply_and_store(i - 1, waiting)
-            waiting = following
-        multiply_and_store(ROUNDS - 1, waiting)
+        quantised = {}
+        accs = {}
+        multiplied = 0
+        for group in tile_groups + [[ROW_TILES - 1 + LAG]]:
+            for t in group:
+                if t < ROW_TILES:
+                    quantised[t] = transpose_and_quantise(t)
+            for t in range(multiplied, min(group[-1] - LAG, ROW_TILES - 1) + 1):
+                i = t // TILES_PER_ROUND
+                if t % TILES_PER_ROUND == 0:
+                    acc = sums.tile([P, BANK], F32, tag="acc")
+                    accs[i] = acc
+                multiply(accs[i], t, quantised[t][0], quantised[t][1])
+                if t % TILES_PER_ROUND == TILES_PER_ROUND - 1:
+                    finish(i, accs[i])
+                multiplied = t + 1

@@ -135,7 +135,8 @@ def tile_parallelretention_pa_kernel(tc, x, Wk, bk, Wv, bv, out):
             nc.vector.tensor_tensor(out=k_and_v[:], in0=acc[:], in1=bias[:], op=ADD)
             halves = k_and_v[:].rearrange("p (t c q) -> p t c q", t=TILES_PER_ROUND, c=2)
             kv = products.tile([P, TILES_PER_ROUND * QD], F32)
-            nc.vector.tensor_tensor(
+            multiplier = nc.vector if i == ROUNDS - 1 else nc.gpsimd
+            multiplier.tensor_tensor(
                 out=kv[:].rearrange("p (t q) -> p t q", t=TILES_PER_ROUND),
                 in0=halves[:, :, 0, :],
                 in1=halves[:, :, 1, :],

@@ -30,13 +30,13 @@ LAG = 2
 FLOPS = 2 * ROWS * E * 2 * QD
 
 
-def transpose_rows(nc, banks, identity, words, copy, grouped_words):
+def transpose_rows(nc, banks, identity, words, copies, grouped_words):
     for h in range(BANKS_PER_TILE):
         bank = banks.tile([P, BANK], F32)
         for j in range(TRANSPOSES_PER_BANK):
             first = (h * TRANSPOSES_PER_BANK + j) * P
             nc.tensor.transpose(bank[:, j * P : (j + 1) * P], words[:, first : first + P], identity[:])
-        copy(
+        copies[h](
             out=grouped_words[:, h * PASSES_PER_BANK : (h + 1) * PASSES_PER_BANK, :, :],
             in_=bank[:].rearrange("p (g u r) -> p g r u", g=PASSES_PER_BANK, u=2),
         )
@@ -86,9 +86,9 @@ def tile_parallelretention_pa_kernel(tc, x, Wk, bk, Wv, bv, out):
 
         w_grouped = const.tile([P, PASSES * 2 * QD * 4], BF16, align_bytes=64)
         w_words = w_grouped[:].bitcast(F32).rearrange("p (g n u) -> p g n u", g=PASSES, u=2)
-        transpose_rows(nc, banks, identity, wk_sb[:].bitcast(F32), nc.scalar.copy, w_words[:, :, 0:QD, :])
+        transpose_rows(nc, banks, identity, wk_sb[:].bitcast(F32), [nc.scalar.copy] * 2, w_words[:, :, 0:QD, :])
         transpose_rows(
-            nc, banks, identity, wv_sb[:].bitcast(F32), nc.vector.tensor_copy, w_words[:, :, QD : 2 * QD, :]
+            nc, banks, identity, wv_sb[:].bitcast(F32), [nc.vector.tensor_copy] * 2, w_words[:, :, QD : 2 * QD, :]
         )
         w_codes = const.tile([P, PASSES * 2 * QD], U32, align_bytes=64)
         w_scales = const.tile([P, PASSES * 2 * QD], U8, align_bytes=64)
@@ -101,18 +101,26 @@ def tile_parallelretention_pa_kernel(tc, x, Wk, bk, Wv, bv, out):
             nc.vector.tensor_copy(out=bias[:, t * 2 * QD : (t + 1) * 2 * QD], in_=bias_sum[:, 0 : 2 * QD])
 
         def transpose_and_quantise(t):
+            shared = t % 4 == 3
             grouped = stage.tile([P, PASSES * P * 4], BF16, align_bytes=64)
             transpose_rows(
                 nc,
                 banks,
                 identity,
                 x_words[t],
-                nc.scalar.copy,
+                [nc.scalar.copy, nc.vector.tensor_copy if shared else nc.scalar.copy],
                 grouped[:].bitcast(F32).rearrange("p (g r u) -> p g r u", g=PASSES, u=2),
             )
             codes = operands.tile([P, PASSES * P], U32, align_bytes=64)
             scales = operands.tile([P, PASSES * P], U8, align_bytes=64)
-            nc.vector.quantize_mx(out=codes[:].bitcast(FP8X4), scales=scales[:], in_=grouped[:])
+            calls = BANKS_PER_TILE if shared else 1
+            width = PASSES * P // calls
+            for c in range(calls):
+                nc.vector.quantize_mx(
+                    out=codes[:, c * width : (c + 1) * width].bitcast(FP8X4),
+                    scales=scales[:, c * width : (c + 1) * width],
+                    in_=grouped[:, c * width * 4 : (c + 1) * width * 4],
+                )
             return codes, scales
 
         def multiply(acc, t, codes, scales):

@@ -47,7 +47,8 @@ def tile_parallelretention_pa_kernel(tc, x, Wk, bk, Wv, bv, out):
     x_rows = x.flatten_outer_dims().rearrange("(p t) e -> p (t e)", t=ROW_TILES)
     out_rows = out.flatten_outer_dims().rearrange("(p t) q -> p (t q)", t=ROW_TILES)
 
-    tile_groups = [[0], [1], [2], [3]] + [[t, t + 1] for t in range(4, ROW_TILES, 2)]
+    load_groups = [[0], [1], [2], [3]] + [[t, t + 1] for t in range(4, ROW_TILES, 2)]
+    tile_groups = [[t] for t in range(ROW_TILES)]
 
     with ExitStack() as ctx:
         const = ctx.enter_context(tc.tile_pool(name="const", bufs=1))
@@ -73,7 +74,7 @@ def tile_parallelretention_pa_kernel(tc, x, Wk, bk, Wv, bv, out):
         wv_sb = const.tile([P, E], BF16)
         nc.sync.dma_start(out=wv_sb[:], in_=Wv)
         x_words = {}
-        for group in tile_groups:
+        for group in load_groups:
             x_sb = x_pool.tile([P, len(group) * E], BF16, tag="x%d" % group[0])
             nc.sync.dma_start(out=x_sb[:], in_=x_rows[:, group[0] * E : (group[-1] + 1) * E])
             for j, t in enumerate(group):

from contextlib import ExitStack

import concourse.mybir as mybir
from concourse.masks import make_identity

F32 = mybir.dt.float32
BF16 = mybir.dt.bfloat16
U32 = mybir.dt.uint32
U8 = mybir.dt.uint8
FP8X4 = mybir.dt.float8_e4m3fn_x4
ADD = mybir.AluOpType.add
MULT = mybir.AluOpType.mult

P = 128
ROWS = 16 * 1 * 128
E = 2048
QD = 128
K_PASS = 4 * P
PASSES = E // K_PASS
WORDS = E // 2
BANK = 512
TRANSPOSES_PER_BANK = BANK // P
BANKS_PER_TILE = WORDS // BANK
PASSES_PER_BANK = PASSES // BANKS_PER_TILE
ROW_TILES = ROWS // P
TILES_PER_ROUND = BANK // (2 * QD)
ROUNDS = ROW_TILES // TILES_PER_ROUND
LAG = 2

FLOPS = 2 * ROWS * E * 2 * QD


def transpose_rows(nc, banks, identity, words, copies, grouped_words):
    for h in range(BANKS_PER_TILE):
        bank = banks.tile([P, BANK], F32)
        for j in range(TRANSPOSES_PER_BANK):
            first = (h * TRANSPOSES_PER_BANK + j) * P
            nc.tensor.transpose(bank[:, j * P : (j + 1) * P], words[:, first : first + P], identity[:])
        copies[h](
            out=grouped_words[:, h * PASSES_PER_BANK : (h + 1) * PASSES_PER_BANK, :, :],
            in_=bank[:].rearrange("p (g u r) -> p g r u", g=PASSES_PER_BANK, u=2),
        )


def tile_parallelretention_pa_kernel(tc, x, Wk, bk, Wv, bv, out):
    nc = tc.nc
    x_rows = x.flatten_outer_dims().rearrange("(p t) e -> p (t e)", t=ROW_TILES)
    out_rows = out.flatten_outer_dims().rearrange("(p t) q -> p (t q)", t=ROW_TILES)

    load_groups = [[0], [1], [2], [3]] + [[t, t + 1] for t in range(4, ROW_TILES, 2)]
    tile_groups = [[t] for t in range(ROW_TILES)]

    with ExitStack() as ctx:
        const = ctx.enter_context(tc.tile_pool(name="const", bufs=1))
        x_pool = ctx.enter_context(tc.tile_pool(name="x_pool", bufs=1))
        stage = ctx.enter_context(tc.tile_pool(name="stage", bufs=2 * TILES_PER_ROUND))
        operands = ctx.enter_context(tc.tile_pool(name="operands", bufs=3 * TILES_PER_ROUND))
        results = ctx.enter_context(tc.tile_pool(name="results", bufs=3))
        products = ctx.enter_context(tc.tile_pool(name="products", bufs=ROUNDS))
        banks = ctx.enter_context(tc.psum_pool(name="banks", bufs=6))
        sums = ctx.enter_context(tc.psum_pool(name="sums", bufs=2))
        ctx.enter_context(tc.manual_schedule())

        bias_rows = const.tile([P, 2 * QD], BF16)
        nc.vector.memset(bias_rows[:], 0.0)
        nc.scalar.dma_start(out=bias_rows[0:1, 0:QD], in_=bk.rearrange("(o q) -> o q", o=1))
        nc.scalar.dma_start(out=bias_rows[0:1, QD : 2 * QD], in_=bv.rearrange("(o q) -> o q", o=1))
        warm_in = const.tile([P, 1], F32)
        nc.vector.memset(warm_in[:], 0.0)
        warm_out = const.tile([P, 1], F32)
        nc.scalar.copy(out=warm_out[:], in_=warm_in[:])
        wk_sb = const.tile([P, E], BF16)
        nc.sync.dma_start(out=wk_sb[:], in_=Wk)
        wv_sb = const.tile([P, E], BF16)
        nc.sync.dma_start(out=wv_sb[:], in_=Wv)
        x_words = {}
        for group in load_groups:
            x_sb = x_pool.tile([P, len(group) * E], BF16, tag="x%d" % group[0])
            nc.sync.dma_start(out=x_sb[:], in_=x_rows[:, group[0] * E : (group[-1] + 1) * E])
            for j, t in enumerate(group):
                x_words[t] = x_sb[:].bitcast(F32)[:, j * WORDS : (j + 1) * WORDS]

        identity = const.tile([P, P], F32)
        make_identity(nc, identity[:])
        ones = const.tile([P, P], BF16)
        nc.vector.memset(ones[:], 1.0)

        w_grouped = const.tile([P, PASSES * 2 * QD * 4], BF16, align_bytes=64)
        w_words = w_grouped[:].bitcast(F32).rearrange("p (g n u) -> p g n u", g=PASSES, u=2)
        transpose_rows(nc, banks, identity, wk_sb[:].bitcast(F32), [nc.scalar.copy] * 2, w_words[:, :, 0:QD, :])
        transpose_rows(
            nc, banks, identity, wv_sb[:].bitcast(F32), [nc.vector.tensor_copy] * 2, w_words[:, :, QD : 2 * QD, :]
        )
        w_codes = const.tile([P, PASSES * 2 * QD], U32, align_bytes=64)
        w_scales = const.tile([P, PASSES * 2 * QD], U8, align_bytes=64)
        nc.vector.quantize_mx(out=w_codes[:].bitcast(FP8X4), scales=w_scales[:], in_=w_grouped[:])

        bias_sum = sums.tile([P, BANK], F32, tag="acc")
        nc.tensor.matmul(out=bias_sum[:, 0 : 2 * QD], lhsT=ones[:], rhs=bias_rows[:], start=True, stop=True)
        bias = const.tile([P, BANK], F32)
        for t in range(TILES_PER_ROUND):
            nc.vector.tensor_copy(out=bias[:, t * 2 * QD : (t + 1) * 2 * QD], in_=bias_sum[:, 0 : 2 * QD])

        def transpose_and_quantise(t):
            shared = t % 4 == 3
            grouped = stage.tile([P, PASSES * P * 4], BF16, align_bytes=64)
            transpose_rows(
                nc,
                banks,
                identity,
                x_words[t],
                [nc.scalar.copy, nc.vector.tensor_copy if shared else nc.scalar.copy],
                grouped[:].bitcast(F32).rearrange("p (g r u) -> p g r u", g=PASSES, u=2),
            )
            codes = operands.tile([P, PASSES * P], U32, align_bytes=64)
            scales = operands.tile([P, PASSES * P], U8, align_bytes=64)
            calls = BANKS_PER_TILE if shared else 1
            width = PASSES * P // calls
            for c in range(calls):
                nc.vector.quantize_mx(
                    out=codes[:, c * width : (c + 1) * width].bitcast(FP8X4),
                    scales=scales[:, c * width : (c + 1) * width],
                    in_=grouped[:, c * width * 4 : (c + 1) * width * 4],
                )
            return codes, scales

        def multiply(acc, t, codes, scales):
            half = t % TILES_PER_ROUND
            for g in range(PASSES):
                rows = slice(g * P, (g + 1) * P)
                cols = slice(g * 2 * QD, (g + 1) * 2 * QD)
                nc.tensor.matmul_mx(
                    out=acc[:, half * 2 * QD : (half + 1) * 2 * QD],
                    lhsT=codes[:, rows].bitcast(FP8X4),
                    lhsT_scale=scales[:, rows],
                    rhs=w_codes[:, cols].bitcast(FP8X4),
                    rhs_scale=w_scales[:, cols],
                    start=(g == 0),
                    stop=(g == PASSES - 1),
                )

        def finish(i, acc):
            k_and_v = results.tile([P, BANK], F32)
            nc.vector.tensor_tensor(out=k_and_v[:], in0=acc[:], in1=bias[:], op=ADD)
            halves = k_and_v[:].rearrange("p (t c q) -> p t c q", t=TILES_PER_ROUND, c=2)
            kv = products.tile([P, TILES_PER_ROUND * QD], F32)
            multiplier = nc.vector if i == ROUNDS - 1 else nc.gpsimd
            multiplier.tensor_tensor(
                out=kv[:].rearrange("p (t q) -> p t q", t=TILES_PER_ROUND),
                in0=halves[:, :, 0, :],
                in1=halves[:, :, 1, :],
                op=MULT,
            )
            nc.sync.dma_start(
                out=out_rows[:, i * TILES_PER_ROUND * QD : (i + 1) * TILES_PER_ROUND * QD], in_=kv[:]
            )

        quantised = {}
        accs = {}
        multiplied = 0
        for group in tile_groups + [[ROW_TILES - 1 + LAG]]:
            for t in group:
                if t < ROW_TILES:
                    quantised[t] = transpose_and_quantise(t)
            for t in range(multiplied, min(group[-1] - LAG, ROW_TILES - 1) + 1):
                i = t // TILES_PER_ROUND
                if t % TILES_PER_ROUND == 0:
                    acc = sums.tile([P, BANK], F32, tag="acc")
                    accs[i] = acc
                multiply(accs[i], t, quantised[t][0], quantised[t][1])
                if t % TILES_PER_ROUND == TILES_PER_ROUND - 1:
                    finish(i, accs[i])
                multiplied = t + 1
